import numpy as np
import ml_dtypes


def mxq(x, axis, fmt="e4m3"):
    dtype, down = {"e4m3": (ml_dtypes.float8_e4m3fn, 7), "e5m2": (ml_dtypes.float8_e5m2, 14)}[fmt]
    v = np.moveaxis(np.asarray(x, np.float32).astype(ml_dtypes.bfloat16).astype(np.float64), axis, -1)
    blocks = v.reshape(v.shape[:-1] + (-1, 32))
    amax = np.abs(blocks).max(-1, keepdims=True)
    byte = np.maximum(np.where(amax > 0, np.frexp(amax)[1] - 1 + 127, 0) - down, 1)
    scale = np.exp2(byte - 127.0)
    codes = (blocks / scale).astype(np.float32).astype(dtype).astype(np.float64)
    return np.moveaxis((codes * scale).reshape(v.shape), -1, axis)


WIDE = False


def mx_kscale(k):
    if not WIDE:
        return np.ones(k)
    levels = np.array([30, -30])
    if k % 512:
        return np.exp2(np.random.permutation(np.resize(levels, k // 32))).repeat(32)
    a = np.empty((k // 512, 16))
    for p in range(k // 512):
        a[p, :8] = np.random.permutation(np.resize(levels, 8))
        for g in range(8):
            far = levels[np.abs(levels - a[p, g]) >= 10]
            a[p, g + 8] = far[np.random.randint(len(far))]
    return np.exp2(a.ravel()).repeat(32)


BF16 = ml_dtypes.bfloat16


def bf(x):
    return np.asarray(x, np.float32).astype(BF16)


def f64(x):
    return np.asarray(x).astype(np.float64)


B, S, POS, NL, H, D, E = 2, 256, 768, 2, 16, 128, 2048
HALF = D // 2


def rope(t, c, s):
    t1 = t[..., :HALF]
    t2 = t[..., HALF:]
    return np.concatenate([c * t1 - s * t2, s * t1 + c * t2], axis=-1)


def setup_inputs():
    g = mx_kscale(E)
    return {"x": bf(np.random.standard_normal((B, S, E)) * g),
            "cos": bf(np.random.uniform(size=(1, S, 1, HALF))),
            "sin": bf(np.random.uniform(size=(1, S, 1, HALF))),
            "Wq": bf(np.random.standard_normal((H * D, E)) * 1.5 / np.sqrt(E) / g),
            "bq": bf(np.random.standard_normal(H * D) * 0.3),
            "Wk": bf(np.random.standard_normal((H * D, E)) * 1.5 / np.sqrt(E) / g),
            "bk": bf(np.random.standard_normal(H * D) * 0.3)}


def reference(x, cos, sin, Wq, bq, Wk, bk):
    xq = mxq(f64(x), 2, "e5m2")
    q = ((xq @ mxq(f64(Wq).T, 0, "e5m2")) + f64(bq)).reshape(B, S, H, D)
    k = ((xq @ mxq(f64(Wk).T, 0, "e5m2")) + f64(bk)).reshape(B, S, H, D)
    return rope(q, f64(cos), f64(sin)), rope(k, f64(cos), f64(sin))

@@ -1,0 +1,321 @@
+from contextlib import ExitStack
+
+import concourse.mybir as mybir
+from concourse.masks import make_identity
+
+B, S, H, D, E = 2, 256, 16, 128, 2048
+FLOPS = 2 * 2 * B * S * E * H * D
+
+F32 = mybir.dt.float32
+BF16 = mybir.dt.bfloat16
+U32 = mybir.dt.uint32
+U8 = mybir.dt.uint8
+E5M2X4 = mybir.dt.float8_e5m2_x4
+ALU = mybir.AluOpType
+
+P = 128
+HALF = D // 2
+K_PASS = 512
+PASSES = E // K_PASS
+N_TILE = 512
+ROW_TILES = N_TILE // P
+HEADS = N_TILE // D
+TOKEN_TILES = B * S // P
+POS_TILES = S // P
+W_TILES = 2 * H * D // N_TILE
+UNITS = W_TILES * TOKEN_TILES
+CHUNK_PASSES = 2
+CHUNKS = W_TILES * PASSES // CHUNK_PASSES
+PASS_WORDS = K_PASS // 2
+
+TRANSPOSE_BANKS = 4
+SUM_BANKS = 3
+RAW_BUFS = 4
+SPLIT_BUFS = 3
+GROUPED_BUFS = 3
+X_GROUPED_BUFS = 2
+CODE_BUFS = 5
+WORK_BUFS = 3
+OUT_BUFS = 6
+SPLIT_ROW_TILES = 2
+QSLOT = 0
+
+
+def tile_selfattention_pa_kernel(tc, x, cos, sin, Wq, bq, Wk, bk, out_0, out_1):
+    nc = tc.nc
+    x_rows = x.rearrange("b s k -> (b s) k")
+    weights = (Wq, Wk)
+    outs = (out_0.rearrange("b s h d -> (b s) (h d)"), out_1.rearrange("b s h d -> (b s) (h d)"))
+    tiles_per_weight = W_TILES // 2
+
+    with ExitStack() as ctx:
+        keep = ctx.enter_context(tc.tile_pool(name="keep", bufs=1))
+        psum = ctx.enter_context(tc.psum_pool(name="psum", bufs=1))
+        ctx.enter_context(tc.manual_schedule())
+
+        count = {}
+
+        def rotating(pool, tag, bufs, shape, dtype):
+            n = count.get(tag, 0)
+            count[tag] = n + 1
+            if pool is psum:
+                return pool.tile(shape, dtype, name="%s%d" % (tag, n), tag="%s%d" % (tag, n % bufs))
+            return pool.tile(shape, dtype, name="%s%d" % (tag, n), tag="%s%d" % (tag, n % bufs), align_bytes=64)
+
+        bias_rows = keep.tile([P, N_TILE], BF16)
+        nc.vector.memset(bias_rows[:], 0.0)
+        rot_rows = keep.tile([P, POS_TILES, 3, HALF], BF16)
+        ident = keep.tile([P, P], F32)
+        make_identity(nc, ident[:])
+        ident_bf16 = keep.tile([P, P], BF16)
+        nc.vector.tensor_copy(out=ident_bf16[:], in_=ident[:])
+
+        rot = psum.tile([P, POS_TILES, 3, HALF], F32, tag="rot")
+        x_raw, x_split, x_grouped, x_codes, x_scales = {}, {}, {}, {}, {}
+        w_raw, w_split, w_grouped, w_codes, w_scales = {}, {}, {}, {}, {}
+        bias, sums, biased, by_cos, by_sin = {}, {}, {}, {}, {}
+
+        def load_x(t):
+            x_raw[t] = keep.tile([P, E], BF16, name="x_raw%d" % t)
+            nc.sync.dma_start(out=x_raw[t][:], in_=x_rows[t * P : (t + 1) * P, :])
+
+        def load_w(first_pass, passes):
+            i, g = divmod(first_pass, PASSES)
+            w, i_in_w = divmod(i, tiles_per_weight)
+            raw = rotating(keep, "w_raw%d_" % passes, RAW_BUFS, [P, ROW_TILES, passes * K_PASS], BF16)
+            rows = weights[w][i_in_w * N_TILE : (i_in_w + 1) * N_TILE, g * K_PASS : (g + passes) * K_PASS]
+            nc.sync.dma_start(out=raw[:], in_=rows.rearrange("(r p) k -> p r k", p=P))
+            for n in range(passes):
+                w_raw[first_pass + n] = (raw[:].rearrange("p r k -> p (r k)").bitcast(F32), passes, n)
+
+        def split_words(words, blocks, copy):
+            split = rotating(keep, "split", SPLIT_BUFS, [P, 2, blocks * P], F32)
+            copy(out=split[:], in_=words[:, 0 : blocks * PASS_WORDS].rearrange("p (m u) -> p u m", u=2))
+            return split
+
+        def split_x(t, copy):
+            x_split[t] = split_words(x_raw[t][:].bitcast(F32), PASSES, copy)
+
+        def split_pass(n, copy):
+            w_split[n] = split_words(w_raw[n][0], ROW_TILES, copy)
+
+        def split_chunk(c):
+            split = split_words(w_raw[CHUNK_PASSES * c][0], SPLIT_ROW_TILES * CHUNK_PASSES, nc.scalar.copy)
+            for n in range(CHUNK_PASSES * c, CHUNK_PASSES * (c + 1)):
+                w_split[n] = split
+
+        def word_pair(words, split, block):
+            if split is not None and block * P < split.shape[2]:
+                return [split[:, u, block * P : (block + 1) * P] for u in range(2)]
+            return [words[:, block * PASS_WORDS + u : (block + 1) * PASS_WORDS : 2] for u in range(2)]
+
+        def transpose_pair(sources, grouped_words, copy):
+            bank = rotating(psum, "transposed", TRANSPOSE_BANKS, [P, 2, 2, P], F32)
+            for a in range(2):
+                for u in range(2):
+                    nc.tensor.transpose(bank[:, a, u, :], sources[a][u], ident[:])
+            copy(out=grouped_words.rearrange("p (a n u) -> p a n u", a=2, u=2), in_=bank[:].rearrange("p a u n -> p a n u"))
+
+        def transpose_x(t, copies):
+            words = x_raw[t][:].bitcast(F32)
+            x_grouped[t] = rotating(keep, "x_grouped", X_GROUPED_BUFS, [P, 4 * N_TILE], BF16)
+            for a in range(2):
+                sources = [word_pair(words, x_split.get(t), g) for g in (2 * a, 2 * a + 1)]
+                transpose_pair(sources, x_grouped[t][:].bitcast(F32)[:, a * N_TILE : (a + 1) * N_TILE], copies[a])
+
+        def transpose_w(n, a, copy):
+            words, passes, place = w_raw[n]
+            c, half = divmod(n, CHUNK_PASSES)
+            if c not in w_grouped:
+                w_grouped[c] = rotating(keep, "w_grouped", GROUPED_BUFS, [P, CHUNK_PASSES, 4 * N_TILE], BF16)
+            sources = [word_pair(words, w_split.get(n), r * passes + place) for r in (2 * a, 2 * a + 1)]
+            transpose_pair(sources, w_grouped[c][:, half, :].bitcast(F32)[:, a * N_TILE : (a + 1) * N_TILE], copy)
+
+        def transpose_pass(n, copies):
+            for a in range(2):
+                transpose_w(n, a, copies[a])
+
+        def transpose_chunk(c):
+            split_chunk(c)
+            for a in (1, 0):
+                for n in range(CHUNK_PASSES * c, CHUNK_PASSES * (c + 1)):
+                    transpose_w(n, a, nc.scalar.copy)
+            if c + RAW_BUFS < CHUNKS:
+                load_w(CHUNK_PASSES * (c + RAW_BUFS), CHUNK_PASSES)
+
+        def quantize_x(t):
+            x_codes[t] = keep.tile([P, PASSES, P], U32, name="x_codes%d" % t, align_bytes=64)
+            x_scales[t] = keep.tile([P, PASSES, P], U8, name="x_scales%d" % t, align_bytes=64)
+            nc.vector.quantize_mx(
+                out=x_codes[t][:].rearrange("p g n -> p (g n)").bitcast(E5M2X4),
+                scales=x_scales[t][:].rearrange("p g n -> p (g n)"),
+                in_=x_grouped[t][:],
+            )
+
+        def quantize_w(c, halves=slice(0, CHUNK_PASSES)):
+            if c not in w_codes:
+                w_codes[c] = rotating(keep, "w_codes", CODE_BUFS, [P, CHUNK_PASSES, N_TILE], U32)
+                w_scales[c] = rotating(keep, "w_scales", CODE_BUFS, [P, CHUNK_PASSES, N_TILE], U8)
+            nc.vector.quantize_mx(
+                out=w_codes[c][:, halves, :].rearrange("p g n -> p (g n)").bitcast(E5M2X4),
+                scales=w_scales[c][:, halves, :].rearrange("p g n -> p (g n)"),
+                in_=w_grouped[c][:, halves, :].rearrange("p g n -> p (g n)"),
+            )
+
+        def spread_bias(i, copy):
+            bank = rotating(psum, "transposed", TRANSPOSE_BANKS, [P, 2, N_TILE], BF16)
+            for a in range(2):
+                pick = ident_bf16[:, i + a : i + a + 1].to_broadcast([P, P])
+                nc.tensor.matmul(bank[:, a, :], lhsT=pick, rhs=bias_rows[:], start=True, stop=True)
+            pair = keep.tile([P, 2, N_TILE], BF16, name="bias%d" % i)
+            copy(out=pair[:], in_=bank[:])
+            for a in range(2):
+                bias[i + a] = pair[:, a, :]
+
+        def place_rotation():
+            nc.vector.tensor_scalar(out=rot_rows[:, :, 1, :], in0=rot_rows[:, :, 2, :], scalar1=-1.0, scalar2=None, op0=ALU.mult)
+            nc.tensor.matmul(
+                rot[:].rearrange("p t a d -> p (t a d)"),
+                lhsT=ident_bf16[:],
+                rhs=rot_rows[:].rearrange("p t a d -> p (t a d)"),
+                start=True,
+                stop=True,
+            )
+
+        def multiply(j, passes=range(PASSES)):
+            i, t = divmod(j, TOKEN_TILES)
+            if j not in sums:
+                sums[j] = rotating(psum, "sums", SUM_BANKS, [P, N_TILE], F32)
+            for g in passes:
+                c, half = divmod(PASSES * i + g, CHUNK_PASSES)
+                nc.tensor.matmul_mx(
+                    out=sums[j][:],
+                    lhsT=x_codes[t][:, g, :].bitcast(E5M2X4),
+                    lhsT_scale=x_scales[t][:, g, :],
+                    rhs=w_codes[c][:, half, :].bitcast(E5M2X4),
+                    rhs_scale=w_scales[c][:, half, :],
+                    start=(g == 0),
+                    stop=(g == PASSES - 1),
+                )
+
+        def add_bias(j):
+            biased[j] = rotating(keep, "biased", WORK_BUFS, [P, N_TILE], F32)
+            nc.vector.tensor_tensor(out=biased[j][:], in0=bias[j // TOKEN_TILES], in1=sums[j][:], op=ALU.add)
+
+        def scale(j):
+            pos = j % POS_TILES
+            by_cos[j] = rotating(keep, "by_cos", WORK_BUFS, [P, N_TILE], F32)
+            nc.vector.tensor_tensor(
+                out=by_cos[j][:].rearrange("p (a d) -> p a d", d=HALF),
+                in0=biased[j][:].rearrange("p (a d) -> p a d", d=HALF),
+                in1=rot[:, pos, 0:1, :].to_broadcast([P, 2 * HEADS, HALF]),
+                op=ALU.mult,
+            )
+            by_sin[j] = rotating(keep, "by_sin", WORK_BUFS, [P, N_TILE], F32)
+            nc.vector.tensor_tensor(
+                out=by_sin[j][:].rearrange("p (h a d) -> p h a d", a=2, d=HALF),
+                in0=biased[j][:].rearrange("p (h a d) -> p h a d", a=2, d=HALF)[:, :, ::-1, :],
+                in1=rot[:, pos : pos + 1, 1:3, :].to_broadcast([P, HEADS, 2, HALF]),
+                op=ALU.mult,
+            )
+
+        def finish(j, engine):
+            i, t = divmod(j, TOKEN_TILES)
+            w, i_in_w = divmod(i, tiles_per_weight)
+            result = rotating(keep, "result", OUT_BUFS, [P, N_TILE], F32)
+            engine.tensor_tensor(out=result[:], in0=by_cos[j][:], in1=by_sin[j][:], op=ALU.add)
+            nc.sync.dma_start(out=outs[w][t * P : (t + 1) * P, i_in_w * N_TILE : (i_in_w + 1) * N_TILE], in_=result[:])
+
+        def rotate(j):
+            scale(j)
+            finish(j, nc.gpsimd)
+
+        nc.sync.dma_start(out=rot_rows[:, :, 0, :], in_=cos.rearrange("o (t p) e d -> p t (o e d)", p=P))
+        nc.sync.dma_start(out=rot_rows[:, :, 2, :], in_=sin.rearrange("o (t p) e d -> p t (o e d)", p=P))
+        nc.sync.dma_start(out=bias_rows[0:tiles_per_weight, :], in_=bq.rearrange("(i n) -> i n", n=N_TILE))
+        nc.sync.dma_start(out=bias_rows[tiles_per_weight:W_TILES, :], in_=bk.rearrange("(i n) -> i n", n=N_TILE))
+        for n in range(SUM_BANKS):
+            load_x(n)
+            load_w(n, 1)
+        load_w(3, 1)
+        load_x(3)
+        for c in range(2, 2 + RAW_BUFS):
+            load_w(CHUNK_PASSES * c, CHUNK_PASSES)
+
+        both = (nc.scalar.copy, nc.vector.tensor_copy)
+        scalar_only = (nc.scalar.copy, nc.scalar.copy)
+        first, second = slice(0, 1), slice(1, 2)
+        place_rotation()
+        spread_bias(0, nc.scalar.copy)
+        split_x(0, nc.vector.tensor_copy)
+        transpose_x(0, scalar_only)
+        split_pass(0, nc.vector.tensor_copy)
+        transpose_pass(0, scalar_only)
+        split_x(1, nc.vector.tensor_copy)
+        quantize_x(0)
+        transpose_x(1, scalar_only)
+        split_pass(1, nc.vector.tensor_copy)
+        quantize_w(0, first)
+        transpose_pass(1, scalar_only)
+        multiply(0, [0])
+        split_x(2, nc.vector.tensor_copy)
+        quantize_x(1)
+        transpose_x(2, scalar_only)
+        multiply(1, [0])
+        split_pass(2, nc.vector.tensor_copy)
+        quantize_w(0, second)
+        transpose_pass(2, scalar_only)
+        multiply(0, [1])
+        multiply(1, [1])
+        split_pass(3, nc.vector.tensor_copy)
+        quantize_x(2)
+        transpose_pass(3, scalar_only)
+        multiply(2, [0, 1])
+        split_x(3, nc.vector.tensor_copy)
+        quantize_w(1, first)
+        transpose_x(3, scalar_only)
+        multiply(0, [2])
+        multiply(1, [2])
+        multiply(2, [2])
+        quantize_w(1, second)
+        multiply(0, [3])
+        multiply(1, [3])
+        multiply(2, [3])
+        quantize_x(3)
+        add_bias(0)
+        add_bias(1)
+        transpose_chunk(2)
+        multiply(3)
+        rotate(0)
+        add_bias(2)
+        scale(1)
+        quantize_w(2)
+        finish(1, nc.gpsimd)
+        transpose_chunk(3)
+        add_bias(3)
+        scale(2)
+        quantize_w(3)
+        finish(2, nc.gpsimd)
+        transpose_chunk(4)
+        multiply(4)
+        add_bias(4)
+        scale(3)
+        quantize_w(4)
+        finish(3, nc.gpsimd)
+
+        for j in range(4, UNITS, 2):
+            c = j // 2 + 3
+            if c < CHUNKS:
+                transpose_chunk(c)
+            if j % (2 * TOKEN_TILES) == 4 and j // TOKEN_TILES + 1 < W_TILES:
+                spread_bias(j // TOKEN_TILES + 1, nc.scalar.copy)
+            for unit in (j, j + 1):
+                if unit + 1 < UNITS:
+                    multiply(unit + 1)
+            for unit in (j, j + 1):
+                if unit + 1 < UNITS:
+                    add_bias(unit + 1)
+                scale(unit)
+                if unit == j + QSLOT and c < CHUNKS:
+                    quantize_w(c)
+                finish(unit, nc.gpsimd if unit + 1 < UNITS else nc.vector)

@@ -32,13 +32,14 @@ TRANSPOSE_BANKS = 4
 SUM_BANKS = 3
 RAW_BUFS = 4
 SPLIT_BUFS = 3
-GROUPED_BUFS = 3
+STAGING_BUFS = 5
+QUANTIZE_AHEAD = 3
 X_GROUPED_BUFS = 2
 CODE_BUFS = 5
-WORK_BUFS = 3
-OUT_BUFS = 6
+WORK_BUFS = 2
 SPLIT_ROW_TILES = 2
-QSLOT = 0
+VECTOR_COS = 448
+PAIRS = UNITS // 2
 
 
 def tile_selfattention_pa_kernel(tc, x, cos, sin, Wq, bq, Wk, bk, out_0, out_1):
@@ -62,6 +63,9 @@ def tile_selfattention_pa_kernel(tc, x, cos, sin, Wq, bq, Wk, bk, out_0, out_1):
                 return pool.tile(shape, dtype, name="%s%d" % (tag, n), tag="%s%d" % (tag, n % bufs))
             return pool.tile(shape, dtype, name="%s%d" % (tag, n), tag="%s%d" % (tag, n % bufs), align_bytes=64)
 
+        def staging(c, shape, dtype):
+            return keep.tile(shape, dtype, name="staging%d" % c, tag="staging%d" % (c % STAGING_BUFS), align_bytes=64)
+
         bias_rows = keep.tile([P, N_TILE], BF16)
         nc.vector.memset(bias_rows[:], 0.0)
         rot_rows = keep.tile([P, POS_TILES, 3, HALF], BF16)
@@ -73,7 +77,7 @@ def tile_selfattention_pa_kernel(tc, x, cos, sin, Wq, bq, Wk, bk, out_0, out_1):
         rot = psum.tile([P, POS_TILES, 3, HALF], F32, tag="rot")
         x_raw, x_split, x_grouped, x_codes, x_scales = {}, {}, {}, {}, {}
         w_raw, w_split, w_grouped, w_codes, w_scales = {}, {}, {}, {}, {}
-        bias, sums, biased, by_cos, by_sin = {}, {}, {}, {}, {}
+        bias, sums, biased, by_cos, by_sin, results = {}, {}, {}, {}, {}, {}
 
         def load_x(t):
             x_raw[t] = keep.tile([P, E], BF16, name="x_raw%d" % t)
@@ -99,8 +103,8 @@ def tile_selfattention_pa_kernel(tc, x, cos, sin, Wq, bq, Wk, bk, out_0, out_1):
         def split_pass(n, copy):
             w_split[n] = split_words(w_raw[n][0], ROW_TILES, copy)
 
-        def split_chunk(c):
-            split = split_words(w_raw[CHUNK_PASSES * c][0], SPLIT_ROW_TILES * CHUNK_PASSES, nc.scalar.copy)
+        def split_chunk(c, row_tiles):
+            split = split_words(w_raw[CHUNK_PASSES * c][0], row_tiles * CHUNK_PASSES, nc.scalar.copy)
             for n in range(CHUNK_PASSES * c, CHUNK_PASSES * (c + 1)):
                 w_split[n] = split
 
@@ -127,7 +131,7 @@ def tile_selfattention_pa_kernel(tc, x, cos, sin, Wq, bq, Wk, bk, out_0, out_1):
             words, passes, place = w_raw[n]
             c, half = divmod(n, CHUNK_PASSES)
             if c not in w_grouped:
-                w_grouped[c] = rotating(keep, "w_grouped", GROUPED_BUFS, [P, CHUNK_PASSES, 4 * N_TILE], BF16)
+                w_grouped[c] = staging(c, [P, CHUNK_PASSES, 4 * N_TILE], BF16)
             sources = [word_pair(words, w_split.get(n), r * passes + place) for r in (2 * a, 2 * a + 1)]
             transpose_pair(sources, w_grouped[c][:, half, :].bitcast(F32)[:, a * N_TILE : (a + 1) * N_TILE], copy)
 
@@ -135,8 +139,9 @@ def tile_selfattention_pa_kernel(tc, x, cos, sin, Wq, bq, Wk, bk, out_0, out_1):
             for a in range(2):
                 transpose_w(n, a, copies[a])
 
-        def transpose_chunk(c):
-            split_chunk(c)
+        def transpose_chunk(c, row_tiles=SPLIT_ROW_TILES):
+            if row_tiles:
+                split_chunk(c, row_tiles)
             for a in (1, 0):
                 for n in range(CHUNK_PASSES * c, CHUNK_PASSES * (c + 1)):
                     transpose_w(n, a, nc.scalar.copy)
@@ -198,37 +203,48 @@ def tile_selfattention_pa_kernel(tc, x, cos, sin, Wq, bq, Wk, bk, out_0, out_1):
                     stop=(g == PASSES - 1),
                 )
 
-        def add_bias(j):
-            biased[j] = rotating(keep, "biased", WORK_BUFS, [P, N_TILE], F32)
-            nc.vector.tensor_tensor(out=biased[j][:], in0=bias[j // TOKEN_TILES], in1=sums[j][:], op=ALU.add)
+        def add_bias(pair):
+            biased[pair] = rotating(keep, "biased", WORK_BUFS, [P, 2, N_TILE], F32)
+            by_cos[pair] = rotating(keep, "by_cos", WORK_BUFS, [P, 2, N_TILE], F32)
+            by_sin[pair] = rotating(keep, "by_sin", WORK_BUFS, [P, 2, N_TILE], F32)
+            for a in range(2):
+                j = 2 * pair + a
+                nc.vector.tensor_tensor(out=biased[pair][:, a, :], in0=bias[j // TOKEN_TILES], in1=sums[j][:], op=ALU.add)
 
-        def scale(j):
-            pos = j % POS_TILES
-            by_cos[j] = rotating(keep, "by_cos", WORK_BUFS, [P, N_TILE], F32)
-            nc.vector.tensor_tensor(
-                out=by_cos[j][:].rearrange("p (a d) -> p a d", d=HALF),
-                in0=biased[j][:].rearrange("p (a d) -> p a d", d=HALF),
-                in1=rot[:, pos, 0:1, :].to_broadcast([P, 2 * HEADS, HALF]),
+        def times_cos(pair, units, width):
+            for a in units:
+                nc.vector.tensor_tensor(
+                    out=by_cos[pair][:, a, 0:width].rearrange("p (b d) -> p b d", d=HALF),
+                    in0=biased[pair][:, a, 0:width].rearrange("p (b d) -> p b d", d=HALF),
+                    in1=rot[:, a, 0:1, :].to_broadcast([P, width // HALF, HALF]),
+                    op=ALU.mult,
+                )
+
+        def times_cos_rest(pair, width):
+            nc.gpsimd.tensor_tensor(
+                out=by_cos[pair][:, :, width:N_TILE].rearrange("p a (b d) -> p a b d", d=HALF),
+                in0=biased[pair][:, :, width:N_TILE].rearrange("p a (b d) -> p a b d", d=HALF),
+                in1=rot_rows[:, :, 0:1, :].to_broadcast([P, 2, (N_TILE - width) // HALF, HALF]),
                 op=ALU.mult,
             )
-            by_sin[j] = rotating(keep, "by_sin", WORK_BUFS, [P, N_TILE], F32)
+
+        def times_sin(pair, units):
+            n = units.stop - units.start
             nc.vector.tensor_tensor(
-                out=by_sin[j][:].rearrange("p (h a d) -> p h a d", a=2, d=HALF),
-                in0=biased[j][:].rearrange("p (h a d) -> p h a d", a=2, d=HALF)[:, :, ::-1, :],
-                in1=rot[:, pos : pos + 1, 1:3, :].to_broadcast([P, HEADS, 2, HALF]),
+                out=by_sin[pair][:, units, :].rearrange("p a (h e) -> p a h e", e=D),
+                in0=biased[pair][:, units, :].rearrange("p a (h b d) -> p (a h) b d", b=2, d=HALF)[:, :, ::-1, :],
+                in1=rot[:, units, 1:3, :].rearrange("p a b d -> p a (b d)").unsqueeze(2).to_broadcast([P, n, HEADS, D]),
                 op=ALU.mult,
             )
 
-        def finish(j, engine):
-            i, t = divmod(j, TOKEN_TILES)
+        def finish(pair, units, engine, after_chunk):
+            i, t = divmod(2 * pair, TOKEN_TILES)
             w, i_in_w = divmod(i, tiles_per_weight)
-            result = rotating(keep, "result", OUT_BUFS, [P, N_TILE], F32)
-            engine.tensor_tensor(out=result[:], in0=by_cos[j][:], in1=by_sin[j][:], op=ALU.add)
-            nc.sync.dma_start(out=outs[w][t * P : (t + 1) * P, i_in_w * N_TILE : (i_in_w + 1) * N_TILE], in_=result[:])
-
-        def rotate(j):
-            scale(j)
-            finish(j, nc.gpsimd)
+            if pair not in results:
+                results[pair] = staging(after_chunk, [P, 2, N_TILE], F32)
+            engine.tensor_tensor(out=results[pair][:, units, :], in0=by_cos[pair][:, units, :], in1=by_sin[pair][:, units, :], op=ALU.add)
+            rows = outs[w][t * P : (t + 2) * P, i_in_w * N_TILE : (i_in_w + 1) * N_TILE]
+            nc.sync.dma_start(out=rows.rearrange("(a p) n -> p a n", p=P)[:, units, :], in_=results[pair][:, units, :])
 
         nc.sync.dma_start(out=rot_rows[:, :, 0, :], in_=cos.rearrange("o (t p) e d -> p t (o e d)", p=P))
         nc.sync.dma_start(out=rot_rows[:, :, 2, :], in_=sin.rearrange("o (t p) e d -> p t (o e d)", p=P))
@@ -283,39 +299,44 @@ def tile_selfattention_pa_kernel(tc, x, cos, sin, Wq, bq, Wk, bk, out_0, out_1):
         multiply(2, [3])
         quantize_x(3)
         add_bias(0)
-        add_bias(1)
         transpose_chunk(2)
         multiply(3)
-        rotate(0)
-        add_bias(2)
-        scale(1)
+        times_cos(0, range(2), N_TILE)
+        times_sin(0, slice(0, 2))
         quantize_w(2)
-        finish(1, nc.gpsimd)
+        finish(0, slice(0, 2), nc.gpsimd, 2)
         transpose_chunk(3)
-        add_bias(3)
-        scale(2)
+        add_bias(1)
+        times_cos(1, range(2), N_TILE)
         quantize_w(3)
-        finish(2, nc.gpsimd)
-        transpose_chunk(4)
+        transpose_chunk(4, 0)
         multiply(4)
-        add_bias(4)
-        scale(3)
+        multiply(5)
+        times_sin(1, slice(0, 2))
         quantize_w(4)
-        finish(3, nc.gpsimd)
+        finish(1, slice(0, 2), nc.gpsimd, 4)
 
-        for j in range(4, UNITS, 2):
-            c = j // 2 + 3
+        for pair in range(2, PAIRS - 1):
+            c = pair + QUANTIZE_AHEAD
+            width = VECTOR_COS if c < CHUNKS else N_TILE
             if c < CHUNKS:
                 transpose_chunk(c)
-            if j % (2 * TOKEN_TILES) == 4 and j // TOKEN_TILES + 1 < W_TILES:
-                spread_bias(j // TOKEN_TILES + 1, nc.scalar.copy)
-            for unit in (j, j + 1):
-                if unit + 1 < UNITS:
-                    multiply(unit + 1)
-            for unit in (j, j + 1):
-                if unit + 1 < UNITS:
-                    add_bias(unit + 1)
-                scale(unit)
-                if unit == j + QSLOT and c < CHUNKS:
-                    quantize_w(c)
-                finish(unit, nc.gpsimd if unit + 1 < UNITS else nc.vector)
+            if pair % 4 == 2 and pair // 2 + 1 < W_TILES:
+                spread_bias(pair // 2 + 1, nc.scalar.copy)
+            add_bias(pair)
+            multiply(2 * pair + 2)
+            multiply(2 * pair + 3)
+            if width < N_TILE:
+                times_cos_rest(pair, width)
+            times_cos(pair, range(2), width)
+            times_sin(pair, slice(0, 2))
+            if c < CHUNKS:
+                quantize_w(c)
+            finish(pair, slice(0, 2), nc.gpsimd, c)
+
+        last = PAIRS - 1
+        add_bias(last)
+        for a, engine in enumerate((nc.gpsimd, nc.vector)):
+            times_cos(last, [a], N_TILE)
+            times_sin(last, slice(a, a + 1))
+            finish(last, slice(a, a + 1), engine, last + QUANTIZE_AHEAD)

@@ -37,8 +37,9 @@ QUANTIZE_AHEAD = 3
 X_GROUPED_BUFS = 2
 CODE_BUFS = 5
 WORK_BUFS = 2
-SPLIT_ROW_TILES = 2
-VECTOR_COS = 448
+SPLIT_BLOCKS = 6
+SPLIT_AHEAD = 2
+VECTOR_COS = 512
 PAIRS = UNITS // 2
 
 
@@ -103,8 +104,8 @@ def tile_selfattention_pa_kernel(tc, x, cos, sin, Wq, bq, Wk, bk, out_0, out_1):
         def split_pass(n, copy):
             w_split[n] = split_words(w_raw[n][0], ROW_TILES, copy)
 
-        def split_chunk(c, row_tiles):
-            split = split_words(w_raw[CHUNK_PASSES * c][0], row_tiles * CHUNK_PASSES, nc.scalar.copy)
+        def split_chunk(c, blocks):
+            split = split_words(w_raw[CHUNK_PASSES * c][0], blocks, nc.scalar.copy)
             for n in range(CHUNK_PASSES * c, CHUNK_PASSES * (c + 1)):
                 w_split[n] = split
 
@@ -139,9 +140,7 @@ def tile_selfattention_pa_kernel(tc, x, cos, sin, Wq, bq, Wk, bk, out_0, out_1):
             for a in range(2):
                 transpose_w(n, a, copies[a])
 
-        def transpose_chunk(c, row_tiles=SPLIT_ROW_TILES):
-            if row_tiles:
-                split_chunk(c, row_tiles)
+        def transpose_chunk(c):
             for a in (1, 0):
                 for n in range(CHUNK_PASSES * c, CHUNK_PASSES * (c + 1)):
                     transpose_w(n, a, nc.scalar.copy)
@@ -299,17 +298,21 @@ def tile_selfattention_pa_kernel(tc, x, cos, sin, Wq, bq, Wk, bk, out_0, out_1):
         multiply(2, [3])
         quantize_x(3)
         add_bias(0)
+        split_chunk(2, 4)
         transpose_chunk(2)
         multiply(3)
         times_cos(0, range(2), N_TILE)
         times_sin(0, slice(0, 2))
         quantize_w(2)
         finish(0, slice(0, 2), nc.gpsimd, 2)
+        split_chunk(3, 4)
         transpose_chunk(3)
         add_bias(1)
         times_cos(1, range(2), N_TILE)
         quantize_w(3)
-        transpose_chunk(4, 0)
+        transpose_chunk(4)
+        split_chunk(5, 4)
+        split_chunk(6, 4)
         multiply(4)
         multiply(5)
         times_sin(1, slice(0, 2))
@@ -321,6 +324,8 @@ def tile_selfattention_pa_kernel(tc, x, cos, sin, Wq, bq, Wk, bk, out_0, out_1):
             width = VECTOR_COS if c < CHUNKS else N_TILE
             if c < CHUNKS:
                 transpose_chunk(c)
+            if c + SPLIT_AHEAD < CHUNKS:
+                split_chunk(c + SPLIT_AHEAD, SPLIT_BLOCKS)
             if pair % 4 == 2 and pair // 2 + 1 < W_TILES:
                 spread_bias(pair // 2 + 1, nc.scalar.copy)
             add_bias(pair)

from contextlib import ExitStack

import concourse.mybir as mybir
from concourse.masks import make_identity

B, S, H, D, E = 2, 256, 16, 128, 2048
FLOPS = 2 * 2 * B * S * E * H * D

F32 = mybir.dt.float32
BF16 = mybir.dt.bfloat16
U32 = mybir.dt.uint32
U8 = mybir.dt.uint8
E5M2X4 = mybir.dt.float8_e5m2_x4
ALU = mybir.AluOpType

P = 128
HALF = D // 2
K_PASS = 512
PASSES = E // K_PASS
N_TILE = 512
ROW_TILES = N_TILE // P
HEADS = N_TILE // D
TOKEN_TILES = B * S // P
POS_TILES = S // P
W_TILES = 2 * H * D // N_TILE
UNITS = W_TILES * TOKEN_TILES
CHUNK_PASSES = 2
CHUNKS = W_TILES * PASSES // CHUNK_PASSES
PASS_WORDS = K_PASS // 2

TRANSPOSE_BANKS = 4
SUM_BANKS = 3
RAW_BUFS = 4
SPLIT_BUFS = 3
STAGING_BUFS = 5
QUANTIZE_AHEAD = 3
X_GROUPED_BUFS = 2
CODE_BUFS = 5
WORK_BUFS = 2
SPLIT_BLOCKS = 6
SPLIT_AHEAD = 2
VECTOR_COS = 512
PAIRS = UNITS // 2


def tile_selfattention_pa_kernel(tc, x, cos, sin, Wq, bq, Wk, bk, out_0, out_1):
    nc = tc.nc
    x_rows = x.rearrange("b s k -> (b s) k")
    weights = (Wq, Wk)
    outs = (out_0.rearrange("b s h d -> (b s) (h d)"), out_1.rearrange("b s h d -> (b s) (h d)"))
    tiles_per_weight = W_TILES // 2

    with ExitStack() as ctx:
        keep = ctx.enter_context(tc.tile_pool(name="keep", bufs=1))
        psum = ctx.enter_context(tc.psum_pool(name="psum", bufs=1))
        ctx.enter_context(tc.manual_schedule())

        count = {}

        def rotating(pool, tag, bufs, shape, dtype):
            n = count.get(tag, 0)
            count[tag] = n + 1
            if pool is psum:
                return pool.tile(shape, dtype, name="%s%d" % (tag, n), tag="%s%d" % (tag, n % bufs))
            return pool.tile(shape, dtype, name="%s%d" % (tag, n), tag="%s%d" % (tag, n % bufs), align_bytes=64)

        def staging(c, shape, dtype):
            return keep.tile(shape, dtype, name="staging%d" % c, tag="staging%d" % (c % STAGING_BUFS), align_bytes=64)

        bias_rows = keep.tile([P, N_TILE], BF16)
        nc.vector.memset(bias_rows[:], 0.0)
        rot_rows = keep.tile([P, POS_TILES, 3, HALF], BF16)
        ident = keep.tile([P, P], F32)
        make_identity(nc, ident[:])
        ident_bf16 = keep.tile([P, P], BF16)
        nc.vector.tensor_copy(out=ident_bf16[:], in_=ident[:])

        rot = psum.tile([P, POS_TILES, 3, HALF], F32, tag="rot")
        x_raw, x_split, x_grouped, x_codes, x_scales = {}, {}, {}, {}, {}
        w_raw, w_split, w_grouped, w_codes, w_scales = {}, {}, {}, {}, {}
        bias, sums, biased, by_cos, by_sin, results = {}, {}, {}, {}, {}, {}

        def load_x(t):
            x_raw[t] = keep.tile([P, E], BF16, name="x_raw%d" % t)
            nc.sync.dma_start(out=x_raw[t][:], in_=x_rows[t * P : (t + 1) * P, :])

        def load_w(first_pass, passes):
            i, g = divmod(first_pass, PASSES)
            w, i_in_w = divmod(i, tiles_per_weight)
            raw = rotating(keep, "w_raw%d_" % passes, RAW_BUFS, [P, ROW_TILES, passes * K_PASS], BF16)
            rows = weights[w][i_in_w * N_TILE : (i_in_w + 1) * N_TILE, g * K_PASS : (g + passes) * K_PASS]
            nc.sync.dma_start(out=raw[:], in_=rows.rearrange("(r p) k -> p r k", p=P))
            for n in range(passes):
                w_raw[first_pass + n] = (raw[:].rearrange("p r k -> p (r k)").bitcast(F32), passes, n)

        def split_words(words, blocks, copy):
            split = rotating(keep, "split", SPLIT_BUFS, [P, 2, blocks * P], F32)
            copy(out=split[:], in_=words[:, 0 : blocks * PASS_WORDS].rearrange("p (m u) -> p u m", u=2))
            return split

        def split_x(t, copy):
            x_split[t] = split_words(x_raw[t][:].bitcast(F32), PASSES, copy)

        def split_pass(n, copy):
            w_split[n] = split_words(w_raw[n][0], ROW_TILES, copy)

        def split_chunk(c, blocks):
            split = split_words(w_raw[CHUNK_PASSES * c][0], blocks, nc.scalar.copy)
            for n in range(CHUNK_PASSES * c, CHUNK_PASSES * (c + 1)):
                w_split[n] = split

        def word_pair(words, split, block):
            if split is not None and block * P < split.shape[2]:
                return [split[:, u, block * P : (block + 1) * P] for u in range(2)]
            return [words[:, block * PASS_WORDS + u : (block + 1) * PASS_WORDS : 2] for u in range(2)]

        def transpose_pair(sources, grouped_words, copy):
            bank = rotating(psum, "transposed", TRANSPOSE_BANKS, [P, 2, 2, P], F32)
            for a in range(2):
                for u in range(2):
                    nc.tensor.transpose(bank[:, a, u, :], sources[a][u], ident[:])
            copy(out=grouped_words.rearrange("p (a n u) -> p a n u", a=2, u=2), in_=bank[:].rearrange("p a u n -> p a n u"))

        def transpose_x(t, copies):
            words = x_raw[t][:].bitcast(F32)
            x_grouped[t] = rotating(keep, "x_grouped", X_GROUPED_BUFS, [P, 4 * N_TILE], BF16)
            for a in range(2):
                sources = [word_pair(words, x_split.get(t), g) for g in (2 * a, 2 * a + 1)]
                transpose_pair(sources, x_grouped[t][:].bitcast(F32)[:, a * N_TILE : (a + 1) * N_TILE], copies[a])

        def transpose_w(n, a, copy):
            words, passes, place = w_raw[n]
            c, half = divmod(n, CHUNK_PASSES)
            if c not in w_grouped:
                w_grouped[c] = staging(c, [P, CHUNK_PASSES, 4 * N_TILE], BF16)
            sources = [word_pair(words, w_split.get(n), r * passes + place) for r in (2 * a, 2 * a + 1)]
            transpose_pair(sources, w_grouped[c][:, half, :].bitcast(F32)[:, a * N_TILE : (a + 1) * N_TILE], copy)

        def transpose_pass(n, copies):
            for a in range(2):
                transpose_w(n, a, copies[a])

        def transpose_chunk(c):
            for a in (1, 0):
                for n in range(CHUNK_PASSES * c, CHUNK_PASSES * (c + 1)):
                    transpose_w(n, a, nc.scalar.copy)
            if c + RAW_BUFS < CHUNKS:
                load_w(CHUNK_PASSES * (c + RAW_BUFS), CHUNK_PASSES)

        def quantize_x(t):
            x_codes[t] = keep.tile([P, PASSES, P], U32, name="x_codes%d" % t, align_bytes=64)
            x_scales[t] = keep.tile([P, PASSES, P], U8, name="x_scales%d" % t, align_bytes=64)
            nc.vector.quantize_mx(
                out=x_codes[t][:].rearrange("p g n -> p (g n)").bitcast(E5M2X4),
                scales=x_scales[t][:].rearrange("p g n -> p (g n)"),
                in_=x_grouped[t][:],
            )

        def quantize_w(c, halves=slice(0, CHUNK_PASSES)):
            if c not in w_codes:
                w_codes[c] = rotating(keep, "w_codes", CODE_BUFS, [P, CHUNK_PASSES, N_TILE], U32)
                w_scales[c] = rotating(keep, "w_scales", CODE_BUFS, [P, CHUNK_PASSES, N_TILE], U8)
            nc.vector.quantize_mx(
                out=w_codes[c][:, halves, :].rearrange("p g n -> p (g n)").bitcast(E5M2X4),
                scales=w_scales[c][:, halves, :].rearrange("p g n -> p (g n)"),
                in_=w_grouped[c][:, halves, :].rearrange("p g n -> p (g n)"),
            )

        def spread_bias(i, copy):
            bank = rotating(psum, "transposed", TRANSPOSE_BANKS, [P, 2, N_TILE], BF16)
            for a in range(2):
                pick = ident_bf16[:, i + a : i + a + 1].to_broadcast([P, P])
                nc.tensor.matmul(bank[:, a, :], lhsT=pick, rhs=bias_rows[:], start=True, stop=True)
            pair = keep.tile([P, 2, N_TILE], BF16, name="bias%d" % i)
            copy(out=pair[:], in_=bank[:])
            for a in range(2):
                bias[i + a] = pair[:, a, :]

        def place_rotation():
            nc.vector.tensor_scalar(out=rot_rows[:, :, 1, :], in0=rot_rows[:, :, 2, :], scalar1=-1.0, scalar2=None, op0=ALU.mult)
            nc.tensor.matmul(
                rot[:].rearrange("p t a d -> p (t a d)"),
                lhsT=ident_bf16[:],
                rhs=rot_rows[:].rearrange("p t a d -> p (t a d)"),
                start=True,
                stop=True,
            )

        def multiply(j, passes=range(PASSES)):
            i, t = divmod(j, TOKEN_TILES)
            if j not in sums:
                sums[j] = rotating(psum, "sums", SUM_BANKS, [P, N_TILE], F32)
            for g in passes:
                c, half = divmod(PASSES * i + g, CHUNK_PASSES)
                nc.tensor.matmul_mx(
                    out=sums[j][:],
                    lhsT=x_codes[t][:, g, :].bitcast(E5M2X4),
                    lhsT_scale=x_scales[t][:, g, :],
                    rhs=w_codes[c][:, half, :].bitcast(E5M2X4),
                    rhs_scale=w_scales[c][:, half, :],
                    start=(g == 0),
                    stop=(g == PASSES - 1),
                )

        def add_bias(pair):
            biased[pair] = rotating(keep, "biased", WORK_BUFS, [P, 2, N_TILE], F32)
            by_cos[pair] = rotating(keep, "by_cos", WORK_BUFS, [P, 2, N_TILE], F32)
            by_sin[pair] = rotating(keep, "by_sin", WORK_BUFS, [P, 2, N_TILE], F32)
            for a in range(2):
                j = 2 * pair + a
                nc.vector.tensor_tensor(out=biased[pair][:, a, :], in0=bias[j // TOKEN_TILES], in1=sums[j][:], op=ALU.add)

        def times_cos(pair, units, width):
            for a in units:
                nc.vector.tensor_tensor(
                    out=by_cos[pair][:, a, 0:width].rearrange("p (b d) -> p b d", d=HALF),
                    in0=biased[pair][:, a, 0:width].rearrange("p (b d) -> p b d", d=HALF),
                    in1=rot[:, a, 0:1, :].to_broadcast([P, width // HALF, HALF]),
                    op=ALU.mult,
                )

        def times_cos_rest(pair, width):
            nc.gpsimd.tensor_tensor(
                out=by_cos[pair][:, :, width:N_TILE].rearrange("p a (b d) -> p a b d", d=HALF),
                in0=biased[pair][:, :, width:N_TILE].rearrange("p a (b d) -> p a b d", d=HALF),
                in1=rot_rows[:, :, 0:1, :].to_broadcast([P, 2, (N_TILE - width) // HALF, HALF]),
                op=ALU.mult,
            )

        def times_sin(pair, units):
            n = units.stop - units.start
            nc.vector.tensor_tensor(
                out=by_sin[pair][:, units, :].rearrange("p a (h e) -> p a h e", e=D),
                in0=biased[pair][:, units, :].rearrange("p a (h b d) -> p (a h) b d", b=2, d=HALF)[:, :, ::-1, :],
                in1=rot[:, units, 1:3, :].rearrange("p a b d -> p a (b d)").unsqueeze(2).to_broadcast([P, n, HEADS, D]),
                op=ALU.mult,
            )

        def finish(pair, units, engine, after_chunk):
            i, t = divmod(2 * pair, TOKEN_TILES)
            w, i_in_w = divmod(i, tiles_per_weight)
            if pair not in results:
                results[pair] = staging(after_chunk, [P, 2, N_TILE], F32)
            engine.tensor_tensor(out=results[pair][:, units, :], in0=by_cos[pair][:, units, :], in1=by_sin[pair][:, units, :], op=ALU.add)
            rows = outs[w][t * P : (t + 2) * P, i_in_w * N_TILE : (i_in_w + 1) * N_TILE]
            nc.sync.dma_start(out=rows.rearrange("(a p) n -> p a n", p=P)[:, units, :], in_=results[pair][:, units, :])

        nc.sync.dma_start(out=rot_rows[:, :, 0, :], in_=cos.rearrange("o (t p) e d -> p t (o e d)", p=P))
        nc.sync.dma_start(out=rot_rows[:, :, 2, :], in_=sin.rearrange("o (t p) e d -> p t (o e d)", p=P))
        nc.sync.dma_start(out=bias_rows[0:tiles_per_weight, :], in_=bq.rearrange("(i n) -> i n", n=N_TILE))
        nc.sync.dma_start(out=bias_rows[tiles_per_weight:W_TILES, :], in_=bk.rearrange("(i n) -> i n", n=N_TILE))
        for n in range(SUM_BANKS):
            load_x(n)
            load_w(n, 1)
        load_w(3, 1)
        load_x(3)
        for c in range(2, 2 + RAW_BUFS):
            load_w(CHUNK_PASSES * c, CHUNK_PASSES)

        both = (nc.scalar.copy, nc.vector.tensor_copy)
        scalar_only = (nc.scalar.copy, nc.scalar.copy)
        first, second = slice(0, 1), slice(1, 2)
        place_rotation()
        spread_bias(0, nc.scalar.copy)
        split_x(0, nc.vector.tensor_copy)
        transpose_x(0, scalar_only)
        split_pass(0, nc.vector.tensor_copy)
        transpose_pass(0, scalar_only)
        split_x(1, nc.vector.tensor_copy)
        quantize_x(0)
        transpose_x(1, scalar_only)
        split_pass(1, nc.vector.tensor_copy)
        quantize_w(0, first)
        transpose_pass(1, scalar_only)
        multiply(0, [0])
        split_x(2, nc.vector.tensor_copy)
        quantize_x(1)
        transpose_x(2, scalar_only)
        multiply(1, [0])
        split_pass(2, nc.vector.tensor_copy)
        quantize_w(0, second)
        transpose_pass(2, scalar_only)
        multiply(0, [1])
        multiply(1, [1])
        split_pass(3, nc.vector.tensor_copy)
        quantize_x(2)
        transpose_pass(3, scalar_only)
        multiply(2, [0, 1])
        split_x(3, nc.vector.tensor_copy)
        quantize_w(1, first)
        transpose_x(3, scalar_only)
        multiply(0, [2])
        multiply(1, [2])
        multiply(2, [2])
        quantize_w(1, second)
        multiply(0, [3])
        multiply(1, [3])
        multiply(2, [3])
        quantize_x(3)
        add_bias(0)
        split_chunk(2, 4)
        transpose_chunk(2)
        multiply(3)
        times_cos(0, range(2), N_TILE)
        times_sin(0, slice(0, 2))
        quantize_w(2)
        finish(0, slice(0, 2), nc.gpsimd, 2)
        split_chunk(3, 4)
        transpose_chunk(3)
        add_bias(1)
        times_cos(1, range(2), N_TILE)
        quantize_w(3)
        transpose_chunk(4)
        split_chunk(5, 4)
        split_chunk(6, 4)
        multiply(4)
        multiply(5)
        times_sin(1, slice(0, 2))
        quantize_w(4)
        finish(1, slice(0, 2), nc.gpsimd, 4)

        for pair in range(2, PAIRS - 1):
            c = pair + QUANTIZE_AHEAD
            width = VECTOR_COS if c < CHUNKS else N_TILE
            if c < CHUNKS:
                transpose_chunk(c)
            if c + SPLIT_AHEAD < CHUNKS:
                split_chunk(c + SPLIT_AHEAD, SPLIT_BLOCKS)
            if pair % 4 == 2 and pair // 2 + 1 < W_TILES:
                spread_bias(pair // 2 + 1, nc.scalar.copy)
            add_bias(pair)
            multiply(2 * pair + 2)
            multiply(2 * pair + 3)
            if width < N_TILE:
                times_cos_rest(pair, width)
            times_cos(pair, range(2), width)
            times_sin(pair, slice(0, 2))
            if c < CHUNKS:
                quantize_w(c)
            finish(pair, slice(0, 2), nc.gpsimd, c)

        last = PAIRS - 1
        add_bias(last)
        for a, engine in enumerate((nc.gpsimd, nc.vector)):
            times_cos(last, [a], N_TILE)
            times_sin(last, slice(a, a + 1))
            finish(last, slice(a, a + 1), engine, last + QUANTIZE_AHEAD)
